import numpy as np
import ml_dtypes


def mxq(x, axis, fmt="e4m3"):
    dtype, down = {"e4m3": (ml_dtypes.float8_e4m3fn, 7), "e5m2": (ml_dtypes.float8_e5m2, 14)}[fmt]
    v = np.moveaxis(np.asarray(x, np.float32).astype(ml_dtypes.bfloat16).astype(np.float64), axis, -1)
    blocks = v.reshape(v.shape[:-1] + (-1, 32))
    amax = np.abs(blocks).max(-1, keepdims=True)
    byte = np.maximum(np.where(amax > 0, np.frexp(amax)[1] - 1 + 127, 0) - down, 1)
    scale = np.exp2(byte - 127.0)
    codes = (blocks / scale).astype(np.float32).astype(dtype).astype(np.float64)
    return np.moveaxis((codes * scale).reshape(v.shape), -1, axis)


WIDE = False


def mx_kscale(k):
    if not WIDE:
        return np.ones(k)
    levels = np.array([18, -18])
    if k % 512:
        return np.exp2(np.random.permutation(np.resize(levels, k // 32))).repeat(32)
    a = np.empty((k // 512, 16))
    for p in range(k // 512):
        a[p, :8] = np.random.permutation(np.resize(levels, 8))
        for g in range(8):
            far = levels[np.abs(levels - a[p, g]) >= 10]
            a[p, g + 8] = far[np.random.randint(len(far))]
    return np.exp2(a.ravel()).repeat(32)


BF16 = ml_dtypes.bfloat16


def bf(x):
    return np.asarray(x, np.float32).astype(BF16)


def f64(x):
    return np.asarray(x).astype(np.float64)


B, C, CI, N = 2, 1024, 512, 1024
EPS = 1e-5


def setup_inputs():
    s = mx_kscale(N)
    u = mx_kscale(C)
    v = mx_kscale(CI)
    r = np.random.standard_normal
    affinity0 = bf(r((B, N, N)) * 0.2)
    g_x0 = bf(r((B, N, CI)))
    w_w0 = bf(r((C, CI)) * 1.5 / (0.2 * np.sqrt(N) * np.sqrt(CI)))
    w_b = bf(r(C) * 0.3)
    bn_gamma = bf(r(C))
    bn_beta = bf(r(C) * 0.5)
    bn_mean = bf(r(C) * 0.5)
    bn_var = bf(np.random.uniform(0.5, 1.5, C))
    x = bf(r((B, C, N)))
    inv_std = 1.0 / np.sqrt(f64(bn_var) + EPS)
    g = bf(r((B, C, N)) * np.exp2(np.random.randint(-6, 1, (B, 1, N))) / s[None, None, :] * u[None, :, None])
    return {"affinity": bf(f64(affinity0) * s[None, :, None]),
            "g_x": bf(f64(g_x0) / v[None, None, :]),
            "w_w": bf(f64(w_w0) * v[None, :] / u[:, None]),
            "w_b": w_b,
            "bn_gamma": bn_gamma,
            "bn_beta": bn_beta,
            "bn_mean": bn_mean,
            "bn_var": bn_var,
            "x": x,
            "inv_std": np.asarray(inv_std, np.float32),
            "grad_out": g}


def reference(affinity, g_x, w_w, w_b, bn_gamma, bn_beta, bn_mean, bn_var, x, inv_std, grad_out):
    dz2 = f64(grad_out) * (f64(bn_gamma) * f64(inv_std))[None, :, None]
    dy = mxq(dz2, 1, "e5m2").transpose(0, 2, 1) @ mxq(f64(w_w), 0, "e4m3")
    daffinity = mxq(dy, 2, "e5m2") @ mxq(f64(g_x), 2, "e4m3").transpose(0, 2, 1)
    dg_x = mxq(f64(affinity), 1, "e4m3").transpose(0, 2, 1) @ mxq(dy, 1, "e5m2")
    return daffinity, dg_x

@@ -1,0 +1,362 @@
+from contextlib import ExitStack
+
+import concourse.mybir as mybir
+from concourse.masks import make_identity
+
+B, C, CI, N = 2, 1024, 512, 1024
+
+F32 = mybir.dt.float32
+BF16 = mybir.dt.bfloat16
+U32 = mybir.dt.uint32
+U8 = mybir.dt.uint8
+E4M3 = mybir.dt.float8_e4m3fn_x4
+E5M2 = mybir.dt.float8_e5m2_x4
+MULT = mybir.AluOpType.mult
+
+P = 128
+PACK = 4
+K_PASS = P * PACK
+W = 512
+HALVES = N // W
+
+FLOPS = 3 * 2 * B * N * N * CI
+BYTES = 2 * (B * C * N + B * N * N + B * N * CI + C * CI + C) + 4 * C + 4 * (B * N * N + B * N * CI)
+
+PLAN = [
+    ("Gi", 0, 0, 0, "V"),
+    ("Wi", 0, "S"),
+    ("Wi", 1, "S"),
+    ("Xt", 0, 0, "S"),
+    ("Xt", 0, 1, "S"),
+    ("Gi", 0, 0, 1, "V"),
+    ("Wq", 1),
+    ("Gq", 0, 0, 1),
+    ("Gi", 0, 1, 0, "S"),
+    ("Gq", 0, 0, 0),
+    ("Wq", 0),
+    ("Gi", 0, 1, 1, "V"),
+    ("Gq", 0, 1, 0),
+    ("F", 0, 0, "S"),
+    ("Gq", 0, 1, 1),
+    ("Ai", 0, 0, 0, "V"),
+    ("Xq", 0, 1),
+    ("Ct", 0, 0, "S"),
+    ("Ri", 0, 0, "S"),
+    ("Xq", 0, 0),
+    ("F", 0, 1, "S"),
+    ("Cq", 0, 0),
+    ("Ct", 0, 1, "S"),
+    ("Gi", 1, 0, 0, "V"),
+    ("Rq", 0, 0),
+    ("Aq", 0, 0, 0),
+    ("O", 0, 0, 0, "SS"),
+    ("Ri", 0, 1, "V"),
+    ("O", 0, 0, 1, "SS"),
+    ("Xt", 1, 0, "S"),
+    ("Gi", 1, 1, 0, "S"),
+    ("Rq", 0, 1),
+    ("Ai", 0, 1, 0, "V"),
+    ("Gi", 1, 0, 1, "V"),
+    ("Aq", 0, 1, 0),
+    ("Gq", 1, 0, 1),
+    ("Gq", 1, 1, 0),
+    ("Gq", 1, 0, 0),
+    ("Xt", 1, 1, "S"),
+    ("O", 0, 1, 3, "SS"),
+    ("Cq", 0, 1),
+    ("O", 0, 1, 1, "SS"),
+    ("F", 1, 0, "S"),
+    ("Gi", 1, 1, 1, "V"),
+    ("Xq", 1, 1),
+    ("O", 0, 0, 2, "SS"),
+    ("O", 0, 1, 0, "SS"),
+    ("Gq", 1, 1, 1),
+    ("Xq", 1, 0),
+    ("S", 0, 0, "S"),
+    ("Ai", 0, 1, 1, "V"),
+    ("S", 0, 2, "V"),
+    ("Ri", 1, 0, "V"),
+    ("O", 0, 1, 2, "SS"),
+    ("Aq", 0, 1, 1),
+    ("Rq", 1, 0),
+    ("O", 0, 0, 3, "SS"),
+    ("Ai", 0, 0, 1, "V"),
+    ("F", 1, 1, "S"),
+    ("O", 1, 0, 2, "VS"),
+    ("Ri", 1, 1, "V"),
+    ("Aq", 0, 0, 1),
+    ("O", 1, 0, 3, "SS"),
+    ("Rq", 1, 1),
+    ("Ai", 1, 0, 1, "V"),
+    ("O", 1, 0, 0, "SS"),
+    ("O", 1, 0, 1, "SS"),
+    ("S", 0, 4, "S"),
+    ("S", 0, 7, "V"),
+    ("O", 1, 1, 3, "SS"),
+    ("S", 0, 1, "S"),
+    ("Ai", 1, 0, 0, "V"),
+    ("O", 1, 1, 0, "SV"),
+    ("Ct", 1, 0, "S"),
+    ("Ai", 1, 1, 1, "V"),
+    ("O", 1, 1, 1, "VS"),
+    ("Ct", 1, 1, "S"),
+    ("S", 0, 6, "S"),
+    ("S", 0, 3, "S"),
+    ("Aq", 1, 0, 1),
+    ("Cq", 1, 0),
+    ("Aq", 1, 1, 1),
+    ("S", 0, 5, "S"),
+    ("Cq", 1, 1),
+    ("Ai", 1, 1, 0, "V"),
+    ("S", 1, 7, "S"),
+    ("S", 1, 5, "V"),
+    ("O", 1, 1, 2, "SS"),
+    ("Aq", 1, 0, 0),
+    ("S", 1, 6, "S"),
+    ("S", 1, 4, "S"),
+    ("Aq", 1, 1, 0),
+    ("S", 1, 0, "S"),
+    ("S", 1, 1, "V"),
+    ("S", 1, 3, "V"),
+    ("S", 1, 2, "S"),
+]
+
+
+def tile_sgcam_pb_v_kernel(
+    tc, affinity, g_x, w_w, w_b, bn_gamma, bn_beta, bn_mean, bn_var, x, inv_std, grad_out, out_0, out_1
+):
+    nc = tc.nc
+    with ExitStack() as ctx:
+        keep = ctx.enter_context(tc.tile_pool(name="keep", bufs=1))
+        raw_pool = ctx.enter_context(tc.tile_pool(name="raw", bufs=4))
+        work = ctx.enter_context(tc.tile_pool(name="work", bufs=3))
+        grouped_pool = ctx.enter_context(tc.tile_pool(name="grouped_pool", bufs=8))
+        codes_pool = ctx.enter_context(tc.tile_pool(name="codes", bufs=4))
+        outs = ctx.enter_context(tc.tile_pool(name="outs", bufs=4))
+        psum_t = ctx.enter_context(tc.psum_pool(name="psum_t", bufs=2))
+        psum = ctx.enter_context(tc.psum_pool(name="psum", bufs=6))
+
+        ctx.enter_context(tc.manual_schedule())
+        gamma = keep.tile([P, C // K_PASS, PACK], BF16)
+        nc.scalar.dma_start(out=gamma[:], in_=bn_gamma.rearrange("(g p j) -> p g j", g=C // K_PASS, j=PACK))
+        rstd = keep.tile([P, C // K_PASS, PACK], F32)
+        nc.scalar.dma_start(out=rstd[:], in_=inv_std.rearrange("(g p j) -> p g j", g=C // K_PASS, j=PACK))
+
+        def load_grad(b, g, cols, tile):
+            src = grad_out[b, g * K_PASS : (g + 1) * K_PASS, cols].rearrange("(p j) n -> p j n", j=PACK)
+            nc.sync.dma_start(out=tile[:, :, cols], in_=src)
+
+        grad = {}
+        for b in range(B):
+            for g in range(2):
+                grad_raw = raw_pool.tile([P, PACK, N], BF16, align_bytes=64)
+                grad[b, g] = grad_raw
+        w_raw = {}
+        gx_raw = {}
+        aff_raw = {}
+
+        def load_w(g):
+            if True:
+                w_in = keep.tile([P, PACK, CI], BF16, name="w_in%d" % g)
+                nc.sync.dma_start(
+                    out=w_in[:], in_=w_w[g * K_PASS : (g + 1) * K_PASS, :].rearrange("(p j) k -> p j k", j=PACK)
+                )
+                w_raw[g] = w_in
+
+        def load_gx(b):
+            for h in range(2):
+                gx_in = raw_pool.tile([P, PACK, CI], BF16, align_bytes=64)
+                nc.sync.dma_start(
+                    out=gx_in[:], in_=g_x[b, h * K_PASS : (h + 1) * K_PASS, :].rearrange("(p i) k -> p i k", i=PACK)
+                )
+                gx_raw[b, h] = gx_in
+
+        def load_aff(b):
+            for g in range(2):
+                aff_in = raw_pool.tile([P, PACK, N], BF16, align_bytes=64)
+                nc.sync.dma_start(
+                    out=aff_in[:],
+                    in_=affinity[b, g * K_PASS : (g + 1) * K_PASS, :].rearrange("(p j) m -> p j m", j=PACK),
+                )
+                aff_raw[b, g] = aff_in
+
+        lo, hi, full = slice(0, W), slice(W, N), slice(0, N)
+        load_w(0)
+        load_grad(0, 0, lo, grad[0, 0])
+        load_w(1)
+        load_grad(0, 1, lo, grad[0, 1])
+        load_gx(0)
+        load_grad(0, 0, hi, grad[0, 0])
+        load_grad(0, 1, hi, grad[0, 1])
+        load_aff(0)
+        load_grad(1, 0, full, grad[1, 0])
+        load_grad(1, 1, full, grad[1, 1])
+        load_gx(1)
+        load_aff(1)
+
+        ident = keep.tile([P, P], F32)
+        make_identity(nc, ident[:])
+        factor = keep.tile([P, C // K_PASS, PACK], F32)
+        nc.vector.tensor_tensor(out=factor[:], in0=gamma[:], in1=rstd[:], op=MULT)
+
+        def copy(engine, out, in_):
+            if engine == "S":
+                nc.scalar.copy(out, in_)
+            else:
+                nc.vector.tensor_copy(out=out, in_=in_)
+
+        def interleave(engine, src, dst):
+            copy(
+                engine,
+                dst.rearrange("p (c i) t -> p c t i", i=4),
+                src.rearrange("p t (c i) -> p c t i", i=4),
+            )
+
+        def quantise(grouped, fmt, tag, bufs):
+            codes = codes_pool.tile([P, W], U32, align_bytes=64, name="codes_" + tag, bufs=bufs)
+            scales = codes_pool.tile([P, W], U8, align_bytes=64, name="scales_" + tag, bufs=bufs)
+            nc.vector.quantize_mx(
+                out=codes[:].bitcast(fmt), scales=scales[:], in_=grouped[:].rearrange("p n t -> p (n t)")
+            )
+            return codes, scales
+
+        def matmul(acc, lhs, lhs_cols, lhs_fmt, rhs, rhs_fmt, start, stop):
+            nc.tensor.matmul_mx(
+                out=acc[:],
+                lhsT=lhs[0][:, lhs_cols].bitcast(lhs_fmt),
+                lhsT_scale=lhs[1][:, lhs_cols],
+                rhs=rhs[0][:].bitcast(rhs_fmt),
+                rhs_scale=rhs[1][:],
+                start=start,
+                stop=stop,
+            )
+
+        dz = {}
+        wq = {}
+        gxq = {}
+        dy = {}
+        dyn = {}
+        affq = {}
+
+        grouped = {}
+
+        def group_grad(b, h, g, engine):
+            cols = slice(h * W, (h + 1) * W)
+            scaled = work.tile([P, PACK, W], BF16, align_bytes=64)
+            for j in range(PACK):
+                nc.vector.tensor_scalar(
+                    out=scaled[:, j, :],
+                    in0=grad[b, g][:, j, cols],
+                    scalar1=factor[:, g, j : j + 1],
+                    scalar2=None,
+                    op0=MULT,
+                )
+            grouped["dz", b, h, g] = new_group()
+            interleave(engine, scaled[:], grouped["dz", b, h, g][:])
+
+        def quantise_grad(b, h, g):
+            dz[b, h, g] = quantise(grouped["dz", b, h, g], E5M2, "dz", 4)
+
+        def new_group():
+            fresh = grouped_pool.tile([P, W, PACK], BF16, align_bytes=64, name="grouped")
+            return fresh
+
+        def group_w(g, engine):
+            grouped["w", g] = new_group()
+            copy(
+                engine,
+                grouped["w", g][:].rearrange("p (t m) j -> p t m j", t=PACK),
+                w_raw[g][:].rearrange("p j (m t) -> p t m j", t=PACK),
+            )
+
+        def quantise_w(g):
+            wq[g] = quantise(grouped["w", g], E4M3, "w", 2)
+
+        def turn(tiles, grouped, engine):
+            for pair in range(2):
+                xt = psum_t.tile([P, 2, 2, P], F32)
+                for i in range(2):
+                    words = tiles[2 * pair + i].bitcast(F32)
+                    for u in range(2):
+                        nc.tensor.transpose(xt[:, i, u, :], words[:, u::2], ident[:])
+                half = grouped[:, 256 * pair : 256 * (pair + 1), :].rearrange("p r t -> p (r t)")
+                copy(
+                    engine,
+                    half.bitcast(F32).rearrange("p (i r u) -> p i r u", i=2, u=2),
+                    xt[:].rearrange("p i u r -> p i r u"),
+                )
+
+        def turn_gx(b, h, engine):
+            grouped["gx", b, h] = new_group()
+            turn([gx_raw[b, h][:, i, :] for i in range(PACK)], grouped["gx", b, h], engine)
+
+        def quantise_gx(b, h):
+            gxq[b, h] = quantise(grouped["gx", b, h], E4M3, "gx", 4)
+
+        def first(b, h, engine):
+            dy_rows = work.tile([P, PACK, W], BF16, align_bytes=64)
+            for t in range(PACK):
+                acc = psum.tile([P, W], F32)
+                for g in range(2):
+                    matmul(acc, wq[g], slice(P * t, P * (t + 1)), E4M3, dz[b, h, g], E5M2, g == 0, g == 1)
+                copy(engine, dy_rows[:, t, :], acc[:])
+            dy[b, h] = dy_rows
+
+        dyq = {}
+
+        def group_dy(b, h, engine):
+            grouped["dy", b, h] = new_group()
+            interleave(engine, dy[b, h][:], grouped["dy", b, h][:])
+
+        def quantise_dy(b, h):
+            dyq[b, h] = quantise(grouped["dy", b, h], E5M2, "dy", 3)
+
+        def rows(b, h, i, evac):
+            if True:
+                result_0 = outs.tile([P, N], F32)
+                for m in range(HALVES):
+                    acc = psum.tile([P, W], F32)
+                    matmul(acc, dyq[b, h], slice(P * i, P * (i + 1)), E5M2, gxq[b, m], E4M3, True, True)
+                    copy(
+                        evac[m],
+                        result_0[:, m * W : (m + 1) * W].rearrange("p (r i) -> p r i", i=PACK),
+                        acc[:].rearrange("p (i r) -> p r i", i=PACK),
+                    )
+                n0 = h * W + i * P
+                nc.sync.dma_start(out=out_0[b, n0 : n0 + P, :], in_=result_0[:])
+
+        def turn_dy(b, h, engine):
+            grouped["dyn", b, h] = new_group()
+            turn([dy[b, h][:, t, :] for t in range(PACK)], grouped["dyn", b, h], engine)
+
+        def quantise_dyn(b, h):
+            dyn[b, h] = quantise(grouped["dyn", b, h], E5M2, "dyn", 4)
+
+        def group_aff(b, g, m, engine):
+            grouped["aff", b, g, m] = new_group()
+            interleave(engine, aff_raw[b, g][:, :, m * W : (m + 1) * W], grouped["aff", b, g, m][:])
+
+        def quantise_aff(b, g, m):
+            affq[b, g, m] = quantise(grouped["aff", b, g, m], E4M3, "aff", 6)
+
+        def sources(b, i, evac):
+            if True:
+                acc = psum.tile([P, W], F32)
+                for g in range(2):
+                    matmul(
+                        acc, affq[b, g, i // PACK], slice(P * (i % PACK), P * (i % PACK + 1)), E4M3,
+                        dyn[b, g], E5M2, g == 0, g == 1,
+                    )
+                result_1 = outs.tile([P, CI], F32, bufs=6)
+                copy(
+                    evac,
+                    result_1[:].rearrange("p (r t) -> p r t", t=PACK),
+                    acc[:].rearrange("p (t r) -> p r t", t=PACK),
+                )
+                nc.sync.dma_start(out=out_1[b, i * P : (i + 1) * P, :], in_=result_1[:])
+
+
+        steps = dict(Gi=group_grad, Gq=quantise_grad, Wi=group_w, Wq=quantise_w, Xt=turn_gx, Xq=quantise_gx, F=first,
+                     Ri=group_dy, Rq=quantise_dy, O=rows, Ct=turn_dy, Cq=quantise_dyn, Ai=group_aff, Aq=quantise_aff, S=sources)
+        for step in PLAN:
+            steps[step[0]](*step[1:])

@@ -17,108 +17,150 @@ P = 128
 PACK = 4
 K_PASS = P * PACK
 W = 512
-HALVES = N // W
+PASSES = 2
 
 FLOPS = 3 * 2 * B * N * N * CI
 BYTES = 2 * (B * C * N + B * N * N + B * N * CI + C * CI + C) + 4 * C + 4 * (B * N * N + B * N * CI)
 
 PLAN = [
-    ("Gi", 0, 0, 0, "V"),
+    ("Pf", 0),
+    ("Lg", 0, 1, 1),
+    ("Gs", 0, 1, 1),
+    ("Lw", 1),
+    ("Wi", 1, "V"),
+    ("Lg", 0, 0, 1),
+    ("Lw", 0),
+    ("Gs", 0, 0, 1),
+    ("Gi", 0, 1, 0, "V"),
+    ("Gi", 0, 1, 1, "S"),
     ("Wi", 0, "S"),
-    ("Wi", 1, "S"),
-    ("Xt", 0, 0, "S"),
-    ("Xt", 0, 1, "S"),
-    ("Gi", 0, 0, 1, "V"),
-    ("Wq", 1),
-    ("Gq", 0, 0, 1),
-    ("Gi", 0, 1, 0, "S"),
-    ("Gq", 0, 0, 0),
+    ("Lg", 0, 1, 0),
+    ("Gs", 0, 1, 0),
+    ("Lg", 0, 0, 0),
+    ("Gq", 0, 1),
     ("Wq", 0),
-    ("Gi", 0, 1, 1, "V"),
-    ("Gq", 0, 1, 0),
-    ("F", 0, 0, "S"),
-    ("Gq", 0, 1, 1),
-    ("Ai", 0, 0, 0, "V"),
-    ("Xq", 0, 1),
-    ("Ct", 0, 0, "S"),
-    ("Ri", 0, 0, "S"),
-    ("Xq", 0, 0),
-    ("F", 0, 1, "S"),
-    ("Cq", 0, 0),
-    ("Ct", 0, 1, "S"),
-    ("Gi", 1, 0, 0, "V"),
-    ("Rq", 0, 0),
-    ("Aq", 0, 0, 0),
-    ("O", 0, 0, 0, "SS"),
-    ("Ri", 0, 1, "V"),
-    ("O", 0, 0, 1, "SS"),
-    ("Xt", 1, 0, "S"),
-    ("Gi", 1, 1, 0, "S"),
-    ("Rq", 0, 1),
-    ("Ai", 0, 1, 0, "V"),
+    ("Lg", 1, 0, 0),
+    ("Lg", 1, 1, 0),
+    ("Gi", 0, 0, 1, "S"),
+    ("F", 0, 1),
+    ("Lx", 0),
+    ("Gs", 1, 0, 0),
+    ("Gs", 0, 0, 0),
+    ("Gi", 0, 0, 0, "V"),
+    ("Gs", 1, 1, 0),
+    ("Xt", 0, 0),
+    ("Xt", 0, 1),
+    ("Gq", 0, 0),
     ("Gi", 1, 0, 1, "V"),
-    ("Aq", 0, 1, 0),
-    ("Gq", 1, 0, 1),
-    ("Gq", 1, 1, 0),
-    ("Gq", 1, 0, 0),
-    ("Xt", 1, 1, "S"),
-    ("O", 0, 1, 3, "SS"),
-    ("Cq", 0, 1),
-    ("O", 0, 1, 1, "SS"),
-    ("F", 1, 0, "S"),
-    ("Gi", 1, 1, 1, "V"),
-    ("Xq", 1, 1),
-    ("O", 0, 0, 2, "SS"),
-    ("O", 0, 1, 0, "SS"),
-    ("Gq", 1, 1, 1),
-    ("Xq", 1, 0),
-    ("S", 0, 0, "S"),
-    ("Ai", 0, 1, 1, "V"),
-    ("S", 0, 2, "V"),
+    ("Xu", 0, 1, "V"),
+    ("Gi", 1, 0, 0, "S"),
+    ("La", 1, 1),
+    ("D", 0, 1, 0, "S"),
+    ("Gi", 1, 1, 1, "S"),
+    ("D", 0, 1, 1, "S"),
+    ("Gq", 1, 0),
+    ("Xu", 0, 0, "S"),
+    ("F", 0, 0),
+    ("Ri", 0, 1, "V"),
+    ("D", 0, 0, 0, "S"),
+    ("D", 0, 0, 1, "S"),
+    ("Lx", 1),
+    ("Xq", 0),
+    ("Ri", 0, 0, "V"),
+    ("Xt", 1, 0),
+    ("Rq", 0, 1),
+    ("F", 1, 0),
+    ("Xu", 1, 0, "S"),
+    ("Gi", 1, 1, 0, "V"),
+    ("Ct", 0, 1),
+    ("D", 1, 0, 0, "S"),
+    ("D", 1, 0, 1, "S"),
+    ("O", 0, 1, 1),
+    ("Cu", 0, 1, "S"),
+    ("Rq", 0, 0),
+    ("La", 0, 0),
+    ("La", 0, 1),
+    ("O", 0, 1, 2),
+    ("Ct", 0, 0),
     ("Ri", 1, 0, "V"),
-    ("O", 0, 1, 2, "SS"),
-    ("Aq", 0, 1, 1),
+    ("O", 0, 0, 2),
+    ("Ai", 0, 0, 0, "V"),
+    ("La", 1, 0),
     ("Rq", 1, 0),
-    ("O", 0, 0, 3, "SS"),
+    ("O", 0, 0, 0),
+    ("Gq", 1, 1),
+    ("Oe", 0, 1, 1, "S"),
+    ("Oe", 0, 1, 2, "S"),
+    ("Xt", 1, 1),
     ("Ai", 0, 0, 1, "V"),
-    ("F", 1, 1, "S"),
-    ("O", 1, 0, 2, "VS"),
+    ("O", 0, 1, 0),
+    ("Cu", 0, 0, "S"),
+    ("Xu", 1, 1, "V"),
+    ("Aq", 0, 0),
+    ("O", 0, 1, 3),
+    ("Oe", 0, 0, 2, "S"),
+    ("Cq", 0, 0),
+    ("Oe", 0, 0, 0, "S"),
+    ("Xq", 1),
+    ("Oe", 0, 1, 3, "S"),
+    ("F", 1, 1),
+    ("Cq", 0, 1),
+    ("Oe", 0, 1, 0, "S"),
+    ("O", 0, 0, 3),
+    ("O", 0, 0, 1),
+    ("Oe", 0, 0, 3, "V"),
+    ("D", 1, 1, 0, "S"),
+    ("O", 1, 0, 3),
+    ("D", 1, 1, 1, "S"),
+    ("Oe", 0, 0, 1, "S"),
+    ("S", 0, 1),
+    ("Ai", 0, 1, 1, "V"),
+    ("Oe", 1, 0, 3, "S"),
+    ("O", 1, 0, 0),
+    ("Ct", 1, 0),
     ("Ri", 1, 1, "V"),
-    ("Aq", 0, 0, 1),
-    ("O", 1, 0, 3, "SS"),
+    ("Ai", 0, 1, 0, "V"),
+    ("S", 0, 0),
     ("Rq", 1, 1),
-    ("Ai", 1, 0, 1, "V"),
-    ("O", 1, 0, 0, "SS"),
-    ("O", 1, 0, 1, "SS"),
-    ("S", 0, 4, "S"),
-    ("S", 0, 7, "V"),
-    ("O", 1, 1, 3, "SS"),
-    ("S", 0, 1, "S"),
-    ("Ai", 1, 0, 0, "V"),
-    ("O", 1, 1, 0, "SV"),
-    ("Ct", 1, 0, "S"),
+    ("O", 1, 0, 2),
+    ("Oe", 1, 0, 0, "S"),
+    ("O", 1, 1, 1),
+    ("Se", 0, 1, "S"),
+    ("Aq", 0, 1),
+    ("Ct", 1, 1),
+    ("O", 1, 1, 2),
     ("Ai", 1, 1, 1, "V"),
-    ("O", 1, 1, 1, "VS"),
-    ("Ct", 1, 1, "S"),
-    ("S", 0, 6, "S"),
-    ("S", 0, 3, "S"),
-    ("Aq", 1, 0, 1),
-    ("Cq", 1, 0),
-    ("Aq", 1, 1, 1),
-    ("S", 0, 5, "S"),
-    ("Cq", 1, 1),
+    ("Cu", 1, 0, "S"),
+    ("Oe", 1, 0, 2, "S"),
+    ("O", 1, 0, 1),
+    ("S", 0, 2),
+    ("Se", 0, 0, "S"),
+    ("S", 0, 3),
     ("Ai", 1, 1, 0, "V"),
-    ("S", 1, 7, "S"),
-    ("S", 1, 5, "V"),
-    ("O", 1, 1, 2, "SS"),
-    ("Aq", 1, 0, 0),
-    ("S", 1, 6, "S"),
-    ("S", 1, 4, "S"),
-    ("Aq", 1, 1, 0),
-    ("S", 1, 0, "S"),
-    ("S", 1, 1, "V"),
-    ("S", 1, 3, "V"),
-    ("S", 1, 2, "S"),
+    ("Cu", 1, 1, "V"),
+    ("O", 1, 1, 3),
+    ("Oe", 1, 1, 1, "S"),
+    ("Oe", 1, 1, 2, "S"),
+    ("Aq", 1, 1),
+    ("Cq", 1, 0),
+    ("Cq", 1, 1),
+    ("Oe", 1, 0, 1, "S"),
+    ("Se", 0, 2, "S"),
+    ("O", 1, 1, 0),
+    ("S", 1, 2),
+    ("S", 1, 3),
+    ("Ai", 1, 0, 1, "V"),
+    ("Se", 0, 3, "S"),
+    ("Ai", 1, 0, 0, "V"),
+    ("Oe", 1, 1, 3, "S"),
+    ("Se", 1, 2, "S"),
+    ("Oe", 1, 1, 0, "S"),
+    ("Aq", 1, 0),
+    ("S", 1, 1),
+    ("Se", 1, 3, "S"),
+    ("Se", 1, 1, "S"),
+    ("S", 1, 0),
+    ("Se", 1, 0, "S"),
 ]
 
 
@@ -128,76 +170,26 @@ def tile_sgcam_pb_v_kernel(
     nc = tc.nc
     with ExitStack() as ctx:
         keep = ctx.enter_context(tc.tile_pool(name="keep", bufs=1))
-        raw_pool = ctx.enter_context(tc.tile_pool(name="raw", bufs=4))
-        work = ctx.enter_context(tc.tile_pool(name="work", bufs=3))
-        grouped_pool = ctx.enter_context(tc.tile_pool(name="grouped_pool", bufs=8))
-        codes_pool = ctx.enter_context(tc.tile_pool(name="codes", bufs=4))
+        raw_pool = ctx.enter_context(tc.tile_pool(name="raw_pool", bufs=7))
+        work = ctx.enter_context(tc.tile_pool(name="work", bufs=2))
+        codes_pool = ctx.enter_context(tc.tile_pool(name="codes_pool", bufs=2))
         outs = ctx.enter_context(tc.tile_pool(name="outs", bufs=4))
-        psum_t = ctx.enter_context(tc.psum_pool(name="psum_t", bufs=2))
-        psum = ctx.enter_context(tc.psum_pool(name="psum", bufs=6))
-
+        psum = ctx.enter_context(tc.psum_pool(name="psum", bufs=8))
         ctx.enter_context(tc.manual_schedule())
-        gamma = keep.tile([P, C // K_PASS, PACK], BF16)
-        nc.scalar.dma_start(out=gamma[:], in_=bn_gamma.rearrange("(g p j) -> p g j", g=C // K_PASS, j=PACK))
-        rstd = keep.tile([P, C // K_PASS, PACK], F32)
-        nc.scalar.dma_start(out=rstd[:], in_=inv_std.rearrange("(g p j) -> p g j", g=C // K_PASS, j=PACK))
 
-        def load_grad(b, g, cols, tile):
-            src = grad_out[b, g * K_PASS : (g + 1) * K_PASS, cols].rearrange("(p j) n -> p j n", j=PACK)
-            nc.sync.dma_start(out=tile[:, :, cols], in_=src)
-
-        grad = {}
-        for b in range(B):
-            for g in range(2):
-                grad_raw = raw_pool.tile([P, PACK, N], BF16, align_bytes=64)
-                grad[b, g] = grad_raw
-        w_raw = {}
-        gx_raw = {}
-        aff_raw = {}
-
-        def load_w(g):
-            if True:
-                w_in = keep.tile([P, PACK, CI], BF16, name="w_in%d" % g)
-                nc.sync.dma_start(
-                    out=w_in[:], in_=w_w[g * K_PASS : (g + 1) * K_PASS, :].rearrange("(p j) k -> p j k", j=PACK)
-                )
-                w_raw[g] = w_in
-
-        def load_gx(b):
-            for h in range(2):
-                gx_in = raw_pool.tile([P, PACK, CI], BF16, align_bytes=64)
-                nc.sync.dma_start(
-                    out=gx_in[:], in_=g_x[b, h * K_PASS : (h + 1) * K_PASS, :].rearrange("(p i) k -> p i k", i=PACK)
-                )
-                gx_raw[b, h] = gx_in
-
-        def load_aff(b):
-            for g in range(2):
-                aff_in = raw_pool.tile([P, PACK, N], BF16, align_bytes=64)
-                nc.sync.dma_start(
-                    out=aff_in[:],
-                    in_=affinity[b, g * K_PASS : (g + 1) * K_PASS, :].rearrange("(p j) m -> p j m", j=PACK),
-                )
-                aff_raw[b, g] = aff_in
-
-        lo, hi, full = slice(0, W), slice(W, N), slice(0, N)
-        load_w(0)
-        load_grad(0, 0, lo, grad[0, 0])
-        load_w(1)
-        load_grad(0, 1, lo, grad[0, 1])
-        load_gx(0)
-        load_grad(0, 0, hi, grad[0, 0])
-        load_grad(0, 1, hi, grad[0, 1])
-        load_aff(0)
-        load_grad(1, 0, full, grad[1, 0])
-        load_grad(1, 1, full, grad[1, 1])
-        load_gx(1)
-        load_aff(1)
-
+        gamma = keep.tile([P, PASSES, PACK], BF16)
+        nc.scalar.dma_start(out=gamma[:], in_=bn_gamma.rearrange("(g p j) -> p g j", g=PASSES, j=PACK))
+        rstd = keep.tile([P, PASSES, PACK], F32)
+        nc.scalar.dma_start(out=rstd[:], in_=inv_std.rearrange("(g p j) -> p g j", g=PASSES, j=PACK))
         ident = keep.tile([P, P], F32)
         make_identity(nc, ident[:])
-        factor = keep.tile([P, C // K_PASS, PACK], F32)
-        nc.vector.tensor_tensor(out=factor[:], in0=gamma[:], in1=rstd[:], op=MULT)
+        factor = keep.tile([P, PASSES, PACK], F32)
+
+        raw = {}
+        grouped = {}
+        q = {}
+        dy = {}
+        open_banks = {}
 
         def copy(engine, out, in_):
             if engine == "S":
@@ -212,151 +204,217 @@ def tile_sgcam_pb_v_kernel(
                 src.rearrange("p t (c i) -> p c t i", i=4),
             )
 
-        def quantise(grouped, fmt, tag, bufs):
-            codes = codes_pool.tile([P, W], U32, align_bytes=64, name="codes_" + tag, bufs=bufs)
-            scales = codes_pool.tile([P, W], U8, align_bytes=64, name="scales_" + tag, bufs=bufs)
-            nc.vector.quantize_mx(
-                out=codes[:].bitcast(fmt), scales=scales[:], in_=grouped[:].rearrange("p n t -> p (n t)")
-            )
-            return codes, scales
+        def group_tile(key, width):
+            bufs = 3 if width == W else 5
+            group = work.tile([P, width, PACK], BF16, align_bytes=64, name="group_%d" % width, bufs=bufs)
+            grouped[key] = group
+            return group
 
-        def matmul(acc, lhs, lhs_cols, lhs_fmt, rhs, rhs_fmt, start, stop):
+        def quantise(key, fmt, bufs):
+            group = grouped[key]
+            width = group.shape[1]
+            codes = codes_pool.tile([P, width], U32, align_bytes=64, name="codes_%s_%d" % (key[0], width), bufs=bufs)
+            scales = codes_pool.tile([P, width], U8, align_bytes=64, name="scales_%s_%d" % (key[0], width), bufs=bufs)
+            nc.vector.quantize_mx(
+                out=codes[:].bitcast(fmt), scales=scales[:], in_=group[:].rearrange("p n t -> p (n t)")
+            )
+            q[key] = (codes, scales)
+
+        def matmul(acc, lhs, lhs_cols, lhs_fmt, rhs, rhs_cols, rhs_fmt, start, stop):
             nc.tensor.matmul_mx(
                 out=acc[:],
                 lhsT=lhs[0][:, lhs_cols].bitcast(lhs_fmt),
                 lhsT_scale=lhs[1][:, lhs_cols],
-                rhs=rhs[0][:].bitcast(rhs_fmt),
-                rhs_scale=rhs[1][:],
+                rhs=rhs[0][:, rhs_cols].bitcast(rhs_fmt),
+                rhs_scale=rhs[1][:, rhs_cols],
                 start=start,
                 stop=stop,
             )
 
-        dz = {}
-        wq = {}
-        gxq = {}
-        dy = {}
-        dyn = {}
-        affq = {}
+        def block(i, width):
+            return slice(i * width, (i + 1) * width)
 
-        grouped = {}
+        def load_raw(key, src):
+            tile_in = raw_pool.tile([P, PACK, N], BF16, align_bytes=64, name="raw_in")
+            raw[key] = tile_in
+            nc.sync.dma_start(out=tile_in[:], in_=src)
 
-        def group_grad(b, h, g, engine):
-            cols = slice(h * W, (h + 1) * W)
-            scaled = work.tile([P, PACK, W], BF16, align_bytes=64)
+        def load_grad(b, g, h):
+            if b == 0:
+                tile_in = raw_pool.tile([P, PACK, W], BF16, align_bytes=64, name="raw_half", bufs=4)
+                src = grad_out[b, block(g, K_PASS), block(h, W)]
+            else:
+                tile_in = raw_pool.tile([P, PACK, N], BF16, align_bytes=64, name="raw_in")
+                src = grad_out[b, block(g, K_PASS), :]
+            raw["grad", b, g, h] = tile_in
+            nc.sync.dma_start(out=tile_in[:], in_=src.rearrange("(p j) n -> p j n", j=PACK))
+
+        def load_w(g):
+            w_in = keep.tile([P, PACK, CI], BF16, name="w_in%d" % g)
+            raw["w", g] = w_in
+            nc.sync.dma_start(out=w_in[:], in_=w_w[block(g, K_PASS), :].rearrange("(p j) k -> p j k", j=PACK))
+
+        def load_gx(b):
+            tile_in = raw_pool.tile([P, 2, PACK, CI], BF16, align_bytes=64, name="raw_in")
+            raw["gx", b] = tile_in
+            nc.sync.dma_start(out=tile_in[:], in_=g_x[b].rearrange("(h p i) k -> p h i k", h=2, i=PACK))
+
+        def load_aff(b, g):
+            load_raw(("aff", b, g), affinity[b, block(g, K_PASS), :].rearrange("(p j) m -> p j m", j=PACK))
+
+        def make_factor(passes):
+            nc.vector.tensor_tensor(out=factor[:], in0=gamma[:], in1=rstd[:], op=MULT)
+
+        def scale_grad(b, g, h):
+            src = raw["grad", b, g, h]
             for j in range(PACK):
                 nc.vector.tensor_scalar(
-                    out=scaled[:, j, :],
-                    in0=grad[b, g][:, j, cols],
+                    out=src[:, j, :],
+                    in0=src[:, j, :],
                     scalar1=factor[:, g, j : j + 1],
                     scalar2=None,
                     op0=MULT,
                 )
-            grouped["dz", b, h, g] = new_group()
-            interleave(engine, scaled[:], grouped["dz", b, h, g][:])
 
-        def quantise_grad(b, h, g):
-            dz[b, h, g] = quantise(grouped["dz", b, h, g], E5M2, "dz", 4)
+        def pass_pair(key):
+            group = grouped.get(key) or group_tile(key, 2 * W)
+            return group
 
-        def new_group():
-            fresh = grouped_pool.tile([P, W, PACK], BF16, align_bytes=64, name="grouped")
-            return fresh
+        def group_grad(b, h, g, engine):
+            src = raw["grad", b, g, h if b == 0 else 0]
+            cols = slice(0, W) if b == 0 else block(h, W)
+            interleave(engine, src[:, :, cols], pass_pair(("dz", b, h))[:, block(g, W), :])
+
+        def quantise_grad(b, h):
+            quantise(("dz", b, h), E5M2, 3)
 
         def group_w(g, engine):
-            grouped["w", g] = new_group()
             copy(
                 engine,
-                grouped["w", g][:].rearrange("p (t m) j -> p t m j", t=PACK),
-                w_raw[g][:].rearrange("p j (m t) -> p t m j", t=PACK),
+                pass_pair(("w",))[:, block(g, W), :].rearrange("p (t m) j -> p t m j", t=PACK),
+                raw["w", g][:].rearrange("p j (m t) -> p t m j", t=PACK),
             )
 
-        def quantise_w(g):
-            wq[g] = quantise(grouped["w", g], E4M3, "w", 2)
+        def quantise_w(passes):
+            quantise(("w",), E4M3, 1)
 
-        def turn(tiles, grouped, engine):
+
+        def turn(key, tiles):
+            banks = []
             for pair in range(2):
-                xt = psum_t.tile([P, 2, 2, P], F32)
+                acc = psum.tile([P, W], F32)
                 for i in range(2):
                     words = tiles[2 * pair + i].bitcast(F32)
                     for u in range(2):
-                        nc.tensor.transpose(xt[:, i, u, :], words[:, u::2], ident[:])
-                half = grouped[:, 256 * pair : 256 * (pair + 1), :].rearrange("p r t -> p (r t)")
+                        nc.tensor.transpose(acc[:, block(2 * i + u, P)], words[:, u::2], ident[:])
+                banks.append(acc)
+            open_banks[key] = banks
+
+        def untangle(key, group, c0, engine):
+            for pair in (1, 0):
+                half = group[:, c0 + 256 * pair : c0 + 256 * (pair + 1), :].rearrange("p r t -> p (r t)")
                 copy(
                     engine,
                     half.bitcast(F32).rearrange("p (i r u) -> p i r u", i=2, u=2),
-                    xt[:].rearrange("p i u r -> p i r u"),
+                    open_banks[key][pair][:].rearrange("p (i u r) -> p i r u", i=2, u=2),
                 )
 
-        def turn_gx(b, h, engine):
-            grouped["gx", b, h] = new_group()
-            turn([gx_raw[b, h][:, i, :] for i in range(PACK)], grouped["gx", b, h], engine)
+        def turn_gx(b, h):
+            turn(("gx", b, h), [raw["gx", b][:, h, i, :] for i in range(PACK)])
 
-        def quantise_gx(b, h):
-            gxq[b, h] = quantise(grouped["gx", b, h], E4M3, "gx", 4)
+        def untangle_gx(b, h, engine):
+            group = grouped.get(("gx", b)) or group_tile(("gx", b), N)
+            untangle(("gx", b, h), group, h * W, engine)
 
-        def first(b, h, engine):
-            dy_rows = work.tile([P, PACK, W], BF16, align_bytes=64)
+        def quantise_gx(b):
+            quantise(("gx", b), E4M3, 2)
+
+
+        def first(b, h):
+            banks = []
             for t in range(PACK):
                 acc = psum.tile([P, W], F32)
-                for g in range(2):
-                    matmul(acc, wq[g], slice(P * t, P * (t + 1)), E4M3, dz[b, h, g], E5M2, g == 0, g == 1)
-                copy(engine, dy_rows[:, t, :], acc[:])
-            dy[b, h] = dy_rows
+                for g in range(PASSES):
+                    matmul(acc, q["w",], slice(g * W + t * P, g * W + (t + 1) * P), E4M3, q["dz", b, h], block(g, W), E5M2, g == 0, g == 1)
+                banks.append(acc)
+            open_banks["dy", b, h] = banks
 
-        dyq = {}
+        def second(b, h, pair, engine):
+            if (b, h) not in dy:
+                dy_rows = work.tile([P, PACK, W], BF16, align_bytes=64, bufs=3)
+                dy[b, h] = dy_rows
+            for t in (2 * pair + 1, 2 * pair):
+                copy(engine, dy[b, h][:, t, :], open_banks["dy", b, h][t][:])
 
         def group_dy(b, h, engine):
-            grouped["dy", b, h] = new_group()
-            interleave(engine, dy[b, h][:], grouped["dy", b, h][:])
+            group = group_tile(("dy", b, h), W)
+            interleave(engine, dy[b, h][:], group[:])
 
         def quantise_dy(b, h):
-            dyq[b, h] = quantise(grouped["dy", b, h], E5M2, "dy", 3)
+            quantise(("dy", b, h), E5M2, 3)
 
-        def rows(b, h, i, evac):
-            if True:
-                result_0 = outs.tile([P, N], F32)
-                for m in range(HALVES):
-                    acc = psum.tile([P, W], F32)
-                    matmul(acc, dyq[b, h], slice(P * i, P * (i + 1)), E5M2, gxq[b, m], E4M3, True, True)
-                    copy(
-                        evac[m],
-                        result_0[:, m * W : (m + 1) * W].rearrange("p (r i) -> p r i", i=PACK),
-                        acc[:].rearrange("p (i r) -> p r i", i=PACK),
-                    )
-                n0 = h * W + i * P
-                nc.sync.dma_start(out=out_0[b, n0 : n0 + P, :], in_=result_0[:])
+        def turn_dy(b, h):
+            turn(("dyn", b, h), [dy[b, h][:, t, :] for t in range(PACK)])
 
-        def turn_dy(b, h, engine):
-            grouped["dyn", b, h] = new_group()
-            turn([dy[b, h][:, t, :] for t in range(PACK)], grouped["dyn", b, h], engine)
+        def untangle_dy(b, h, engine):
+            group = group_tile(("dyn", b, h), W)
+            untangle(("dyn", b, h), group, 0, engine)
 
         def quantise_dyn(b, h):
-            dyn[b, h] = quantise(grouped["dyn", b, h], E5M2, "dyn", 4)
+            quantise(("dyn", b, h), E5M2, 4)
 
-        def group_aff(b, g, m, engine):
-            grouped["aff", b, g, m] = new_group()
-            interleave(engine, aff_raw[b, g][:, :, m * W : (m + 1) * W], grouped["aff", b, g, m][:])
+        def group_aff(b, m, g, engine):
+            interleave(engine, raw["aff", b, g][:, :, block(m, W)], pass_pair(("aff", b, m))[:, block(g, W), :])
 
-        def quantise_aff(b, g, m):
-            affq[b, g, m] = quantise(grouped["aff", b, g, m], E4M3, "aff", 6)
+        def quantise_aff(b, m):
+            quantise(("aff", b, m), E4M3, 3)
 
-        def sources(b, i, evac):
-            if True:
+        def rows(b, h, i):
+            banks = []
+            for m in range(2):
                 acc = psum.tile([P, W], F32)
-                for g in range(2):
-                    matmul(
-                        acc, affq[b, g, i // PACK], slice(P * (i % PACK), P * (i % PACK + 1)), E4M3,
-                        dyn[b, g], E5M2, g == 0, g == 1,
-                    )
-                result_1 = outs.tile([P, CI], F32, bufs=6)
+                matmul(acc, q["dy", b, h], block(i, P), E5M2, q["gx", b], block(m, W), E4M3, True, True)
+                banks.append(acc)
+            open_banks["rows", b, h, i] = banks
+
+        def store_rows(b, h, i, engine):
+            result_0 = outs.tile([P, N], F32, bufs=4)
+            for m in (1, 0):
                 copy(
-                    evac,
-                    result_1[:].rearrange("p (r t) -> p r t", t=PACK),
-                    acc[:].rearrange("p (t r) -> p r t", t=PACK),
+                    engine,
+                    result_0[:, block(m, W)].rearrange("p (r i) -> p r i", i=PACK),
+                    open_banks["rows", b, h, i][m][:].rearrange("p (i r) -> p r i", i=PACK),
                 )
-                nc.sync.dma_start(out=out_1[b, i * P : (i + 1) * P, :], in_=result_1[:])
+            nc.sync.dma_start(out=out_0[b, block(h * PACK + i, P), :], in_=result_0[:])
 
+        def sources(b, pair):
+            banks = []
+            for i in range(2):
+                acc = psum.tile([P, W], F32)
+                for g in range(PASSES):
+                    c0 = g * W + (2 * pair + i) % PACK * P
+                    matmul(acc, q["aff", b, pair // 2], slice(c0, c0 + P), E4M3, q["dyn", b, g], slice(0, W), E5M2, g == 0, g == 1)
+                banks.append(acc)
+            open_banks["sources", b, pair] = banks
 
-        steps = dict(Gi=group_grad, Gq=quantise_grad, Wi=group_w, Wq=quantise_w, Xt=turn_gx, Xq=quantise_gx, F=first,
-                     Ri=group_dy, Rq=quantise_dy, O=rows, Ct=turn_dy, Cq=quantise_dyn, Ai=group_aff, Aq=quantise_aff, S=sources)
+        def store_sources(b, pair, engine):
+            result_1 = outs.tile([P, 2, CI], F32, bufs=3)
+            dst = out_1[b, block(pair, 2 * P), :].rearrange("(i p) c -> p i c", i=2)
+            for i in (1, 0):
+                copy(
+                    engine,
+                    result_1[:, i, :].rearrange("p (r t) -> p r t", t=PACK),
+                    open_banks["sources", b, pair][i][:].rearrange("p (t r) -> p r t", t=PACK),
+                )
+                if b == 1:
+                    nc.sync.dma_start(out=dst[:, i, :], in_=result_1[:, i, :])
+            if b == 0:
+                nc.sync.dma_start(out=dst, in_=result_1[:])
+
+        steps = dict(
+            Pf=make_factor, Lg=load_grad, Lw=load_w, Lx=load_gx, La=load_aff, Gs=scale_grad, Gi=group_grad, Gq=quantise_grad, Wi=group_w, Wq=quantise_w, Xt=turn_gx, Xu=untangle_gx,
+            Xq=quantise_gx, F=first, D=second, Ri=group_dy, Rq=quantise_dy, Ct=turn_dy, Cu=untangle_dy, Cq=quantise_dyn,
+            Ai=group_aff, Aq=quantise_aff, O=rows, Oe=store_rows, S=sources, Se=store_sources,
+        )
         for step in PLAN:
             steps[step[0]](*step[1:])

from contextlib import ExitStack

import concourse.mybir as mybir
from concourse.masks import make_identity

B, C, CI, N = 2, 1024, 512, 1024

F32 = mybir.dt.float32
BF16 = mybir.dt.bfloat16
U32 = mybir.dt.uint32
U8 = mybir.dt.uint8
E4M3 = mybir.dt.float8_e4m3fn_x4
E5M2 = mybir.dt.float8_e5m2_x4
MULT = mybir.AluOpType.mult

P = 128
PACK = 4
K_PASS = P * PACK
W = 512
PASSES = 2

FLOPS = 3 * 2 * B * N * N * CI
BYTES = 2 * (B * C * N + B * N * N + B * N * CI + C * CI + C) + 4 * C + 4 * (B * N * N + B * N * CI)

PLAN = [
    ("Pf", 0),
    ("Lg", 0, 1, 1),
    ("Gs", 0, 1, 1),
    ("Lw", 1),
    ("Wi", 1, "V"),
    ("Lg", 0, 0, 1),
    ("Lw", 0),
    ("Gs", 0, 0, 1),
    ("Gi", 0, 1, 0, "V"),
    ("Gi", 0, 1, 1, "S"),
    ("Wi", 0, "S"),
    ("Lg", 0, 1, 0),
    ("Gs", 0, 1, 0),
    ("Lg", 0, 0, 0),
    ("Gq", 0, 1),
    ("Wq", 0),
    ("Lg", 1, 0, 0),
    ("Lg", 1, 1, 0),
    ("Gi", 0, 0, 1, "S"),
    ("F", 0, 1),
    ("Lx", 0),
    ("Gs", 1, 0, 0),
    ("Gs", 0, 0, 0),
    ("Gi", 0, 0, 0, "V"),
    ("Gs", 1, 1, 0),
    ("Xt", 0, 0),
    ("Xt", 0, 1),
    ("Gq", 0, 0),
    ("Gi", 1, 0, 1, "V"),
    ("Xu", 0, 1, "V"),
    ("Gi", 1, 0, 0, "S"),
    ("La", 1, 1),
    ("D", 0, 1, 0, "S"),
    ("Gi", 1, 1, 1, "S"),
    ("D", 0, 1, 1, "S"),
    ("Gq", 1, 0),
    ("Xu", 0, 0, "S"),
    ("F", 0, 0),
    ("Ri", 0, 1, "V"),
    ("D", 0, 0, 0, "S"),
    ("D", 0, 0, 1, "S"),
    ("Lx", 1),
    ("Xq", 0),
    ("Ri", 0, 0, "V"),
    ("Xt", 1, 0),
    ("Rq", 0, 1),
    ("F", 1, 0),
    ("Xu", 1, 0, "S"),
    ("Gi", 1, 1, 0, "V"),
    ("Ct", 0, 1),
    ("D", 1, 0, 0, "S"),
    ("D", 1, 0, 1, "S"),
    ("O", 0, 1, 1),
    ("Cu", 0, 1, "S"),
    ("Rq", 0, 0),
    ("La", 0, 0),
    ("La", 0, 1),
    ("O", 0, 1, 2),
    ("Ct", 0, 0),
    ("Ri", 1, 0, "V"),
    ("O", 0, 0, 2),
    ("Ai", 0, 0, 0, "V"),
    ("La", 1, 0),
    ("Rq", 1, 0),
    ("O", 0, 0, 0),
    ("Gq", 1, 1),
    ("Oe", 0, 1, 1, "S"),
    ("Oe", 0, 1, 2, "S"),
    ("Xt", 1, 1),
    ("Ai", 0, 0, 1, "V"),
    ("O", 0, 1, 0),
    ("Cu", 0, 0, "S"),
    ("Xu", 1, 1, "V"),
    ("Aq", 0, 0),
    ("O", 0, 1, 3),
    ("Oe", 0, 0, 2, "S"),
    ("Cq", 0, 0),
    ("Oe", 0, 0, 0, "S"),
    ("Xq", 1),
    ("Oe", 0, 1, 3, "S"),
    ("F", 1, 1),
    ("Cq", 0, 1),
    ("Oe", 0, 1, 0, "S"),
    ("O", 0, 0, 3),
    ("O", 0, 0, 1),
    ("Oe", 0, 0, 3, "V"),
    ("D", 1, 1, 0, "S"),
    ("O", 1, 0, 3),
    ("D", 1, 1, 1, "S"),
    ("Oe", 0, 0, 1, "S"),
    ("S", 0, 1),
    ("Ai", 0, 1, 1, "V"),
    ("Oe", 1, 0, 3, "S"),
    ("O", 1, 0, 0),
    ("Ct", 1, 0),
    ("Ri", 1, 1, "V"),
    ("Ai", 0, 1, 0, "V"),
    ("S", 0, 0),
    ("Rq", 1, 1),
    ("O", 1, 0, 2),
    ("Oe", 1, 0, 0, "S"),
    ("O", 1, 1, 1),
    ("Se", 0, 1, "S"),
    ("Aq", 0, 1),
    ("Ct", 1, 1),
    ("O", 1, 1, 2),
    ("Ai", 1, 1, 1, "V"),
    ("Cu", 1, 0, "S"),
    ("Oe", 1, 0, 2, "S"),
    ("O", 1, 0, 1),
    ("S", 0, 2),
    ("Se", 0, 0, "S"),
    ("S", 0, 3),
    ("Ai", 1, 1, 0, "V"),
    ("Cu", 1, 1, "V"),
    ("O", 1, 1, 3),
    ("Oe", 1, 1, 1, "S"),
    ("Oe", 1, 1, 2, "S"),
    ("Aq", 1, 1),
    ("Cq", 1, 0),
    ("Cq", 1, 1),
    ("Oe", 1, 0, 1, "S"),
    ("Se", 0, 2, "S"),
    ("O", 1, 1, 0),
    ("S", 1, 2),
    ("S", 1, 3),
    ("Ai", 1, 0, 1, "V"),
    ("Se", 0, 3, "S"),
    ("Ai", 1, 0, 0, "V"),
    ("Oe", 1, 1, 3, "S"),
    ("Se", 1, 2, "S"),
    ("Oe", 1, 1, 0, "S"),
    ("Aq", 1, 0),
    ("S", 1, 1),
    ("Se", 1, 3, "S"),
    ("Se", 1, 1, "S"),
    ("S", 1, 0),
    ("Se", 1, 0, "S"),
]


def tile_sgcam_pb_v_kernel(
    tc, affinity, g_x, w_w, w_b, bn_gamma, bn_beta, bn_mean, bn_var, x, inv_std, grad_out, out_0, out_1
):
    nc = tc.nc
    with ExitStack() as ctx:
        keep = ctx.enter_context(tc.tile_pool(name="keep", bufs=1))
        raw_pool = ctx.enter_context(tc.tile_pool(name="raw_pool", bufs=7))
        work = ctx.enter_context(tc.tile_pool(name="work", bufs=2))
        codes_pool = ctx.enter_context(tc.tile_pool(name="codes_pool", bufs=2))
        outs = ctx.enter_context(tc.tile_pool(name="outs", bufs=4))
        psum = ctx.enter_context(tc.psum_pool(name="psum", bufs=8))
        ctx.enter_context(tc.manual_schedule())

        gamma = keep.tile([P, PASSES, PACK], BF16)
        nc.scalar.dma_start(out=gamma[:], in_=bn_gamma.rearrange("(g p j) -> p g j", g=PASSES, j=PACK))
        rstd = keep.tile([P, PASSES, PACK], F32)
        nc.scalar.dma_start(out=rstd[:], in_=inv_std.rearrange("(g p j) -> p g j", g=PASSES, j=PACK))
        ident = keep.tile([P, P], F32)
        make_identity(nc, ident[:])
        factor = keep.tile([P, PASSES, PACK], F32)

        raw = {}
        grouped = {}
        q = {}
        dy = {}
        open_banks = {}

        def copy(engine, out, in_):
            if engine == "S":
                nc.scalar.copy(out, in_)
            else:
                nc.vector.tensor_copy(out=out, in_=in_)

        def interleave(engine, src, dst):
            copy(
                engine,
                dst.rearrange("p (c i) t -> p c t i", i=4),
                src.rearrange("p t (c i) -> p c t i", i=4),
            )

        def group_tile(key, width):
            bufs = 3 if width == W else 5
            group = work.tile([P, width, PACK], BF16, align_bytes=64, name="group_%d" % width, bufs=bufs)
            grouped[key] = group
            return group

        def quantise(key, fmt, bufs):
            group = grouped[key]
            width = group.shape[1]
            codes = codes_pool.tile([P, width], U32, align_bytes=64, name="codes_%s_%d" % (key[0], width), bufs=bufs)
            scales = codes_pool.tile([P, width], U8, align_bytes=64, name="scales_%s_%d" % (key[0], width), bufs=bufs)
            nc.vector.quantize_mx(
                out=codes[:].bitcast(fmt), scales=scales[:], in_=group[:].rearrange("p n t -> p (n t)")
            )
            q[key] = (codes, scales)

        def matmul(acc, lhs, lhs_cols, lhs_fmt, rhs, rhs_cols, rhs_fmt, start, stop):
            nc.tensor.matmul_mx(
                out=acc[:],
                lhsT=lhs[0][:, lhs_cols].bitcast(lhs_fmt),
                lhsT_scale=lhs[1][:, lhs_cols],
                rhs=rhs[0][:, rhs_cols].bitcast(rhs_fmt),
                rhs_scale=rhs[1][:, rhs_cols],
                start=start,
                stop=stop,
            )

        def block(i, width):
            return slice(i * width, (i + 1) * width)

        def load_raw(key, src):
            tile_in = raw_pool.tile([P, PACK, N], BF16, align_bytes=64, name="raw_in")
            raw[key] = tile_in
            nc.sync.dma_start(out=tile_in[:], in_=src)

        def load_grad(b, g, h):
            if b == 0:
                tile_in = raw_pool.tile([P, PACK, W], BF16, align_bytes=64, name="raw_half", bufs=4)
                src = grad_out[b, block(g, K_PASS), block(h, W)]
            else:
                tile_in = raw_pool.tile([P, PACK, N], BF16, align_bytes=64, name="raw_in")
                src = grad_out[b, block(g, K_PASS), :]
            raw["grad", b, g, h] = tile_in
            nc.sync.dma_start(out=tile_in[:], in_=src.rearrange("(p j) n -> p j n", j=PACK))

        def load_w(g):
            w_in = keep.tile([P, PACK, CI], BF16, name="w_in%d" % g)
            raw["w", g] = w_in
            nc.sync.dma_start(out=w_in[:], in_=w_w[block(g, K_PASS), :].rearrange("(p j) k -> p j k", j=PACK))

        def load_gx(b):
            tile_in = raw_pool.tile([P, 2, PACK, CI], BF16, align_bytes=64, name="raw_in")
            raw["gx", b] = tile_in
            nc.sync.dma_start(out=tile_in[:], in_=g_x[b].rearrange("(h p i) k -> p h i k", h=2, i=PACK))

        def load_aff(b, g):
            load_raw(("aff", b, g), affinity[b, block(g, K_PASS), :].rearrange("(p j) m -> p j m", j=PACK))

        def make_factor(passes):
            nc.vector.tensor_tensor(out=factor[:], in0=gamma[:], in1=rstd[:], op=MULT)

        def scale_grad(b, g, h):
            src = raw["grad", b, g, h]
            for j in range(PACK):
                nc.vector.tensor_scalar(
                    out=src[:, j, :],
                    in0=src[:, j, :],
                    scalar1=factor[:, g, j : j + 1],
                    scalar2=None,
                    op0=MULT,
                )

        def pass_pair(key):
            group = grouped.get(key) or group_tile(key, 2 * W)
            return group

        def group_grad(b, h, g, engine):
            src = raw["grad", b, g, h if b == 0 else 0]
            cols = slice(0, W) if b == 0 else block(h, W)
            interleave(engine, src[:, :, cols], pass_pair(("dz", b, h))[:, block(g, W), :])

        def quantise_grad(b, h):
            quantise(("dz", b, h), E5M2, 3)

        def group_w(g, engine):
            copy(
                engine,
                pass_pair(("w",))[:, block(g, W), :].rearrange("p (t m) j -> p t m j", t=PACK),
                raw["w", g][:].rearrange("p j (m t) -> p t m j", t=PACK),
            )

        def quantise_w(passes):
            quantise(("w",), E4M3, 1)


        def turn(key, tiles):
            banks = []
            for pair in range(2):
                acc = psum.tile([P, W], F32)
                for i in range(2):
                    words = tiles[2 * pair + i].bitcast(F32)
                    for u in range(2):
                        nc.tensor.transpose(acc[:, block(2 * i + u, P)], words[:, u::2], ident[:])
                banks.append(acc)
            open_banks[key] = banks

        def untangle(key, group, c0, engine):
            for pair in (1, 0):
                half = group[:, c0 + 256 * pair : c0 + 256 * (pair + 1), :].rearrange("p r t -> p (r t)")
                copy(
                    engine,
                    half.bitcast(F32).rearrange("p (i r u) -> p i r u", i=2, u=2),
                    open_banks[key][pair][:].rearrange("p (i u r) -> p i r u", i=2, u=2),
                )

        def turn_gx(b, h):
            turn(("gx", b, h), [raw["gx", b][:, h, i, :] for i in range(PACK)])

        def untangle_gx(b, h, engine):
            group = grouped.get(("gx", b)) or group_tile(("gx", b), N)
            untangle(("gx", b, h), group, h * W, engine)

        def quantise_gx(b):
            quantise(("gx", b), E4M3, 2)


        def first(b, h):
            banks = []
            for t in range(PACK):
                acc = psum.tile([P, W], F32)
                for g in range(PASSES):
                    matmul(acc, q["w",], slice(g * W + t * P, g * W + (t + 1) * P), E4M3, q["dz", b, h], block(g, W), E5M2, g == 0, g == 1)
                banks.append(acc)
            open_banks["dy", b, h] = banks

        def second(b, h, pair, engine):
            if (b, h) not in dy:
                dy_rows = work.tile([P, PACK, W], BF16, align_bytes=64, bufs=3)
                dy[b, h] = dy_rows
            for t in (2 * pair + 1, 2 * pair):
                copy(engine, dy[b, h][:, t, :], open_banks["dy", b, h][t][:])

        def group_dy(b, h, engine):
            group = group_tile(("dy", b, h), W)
            interleave(engine, dy[b, h][:], group[:])

        def quantise_dy(b, h):
            quantise(("dy", b, h), E5M2, 3)

        def turn_dy(b, h):
            turn(("dyn", b, h), [dy[b, h][:, t, :] for t in range(PACK)])

        def untangle_dy(b, h, engine):
            group = group_tile(("dyn", b, h), W)
            untangle(("dyn", b, h), group, 0, engine)

        def quantise_dyn(b, h):
            quantise(("dyn", b, h), E5M2, 4)

        def group_aff(b, m, g, engine):
            interleave(engine, raw["aff", b, g][:, :, block(m, W)], pass_pair(("aff", b, m))[:, block(g, W), :])

        def quantise_aff(b, m):
            quantise(("aff", b, m), E4M3, 3)

        def rows(b, h, i):
            banks = []
            for m in range(2):
                acc = psum.tile([P, W], F32)
                matmul(acc, q["dy", b, h], block(i, P), E5M2, q["gx", b], block(m, W), E4M3, True, True)
                banks.append(acc)
            open_banks["rows", b, h, i] = banks

        def store_rows(b, h, i, engine):
            result_0 = outs.tile([P, N], F32, bufs=4)
            for m in (1, 0):
                copy(
                    engine,
                    result_0[:, block(m, W)].rearrange("p (r i) -> p r i", i=PACK),
                    open_banks["rows", b, h, i][m][:].rearrange("p (i r) -> p r i", i=PACK),
                )
            nc.sync.dma_start(out=out_0[b, block(h * PACK + i, P), :], in_=result_0[:])

        def sources(b, pair):
            banks = []
            for i in range(2):
                acc = psum.tile([P, W], F32)
                for g in range(PASSES):
                    c0 = g * W + (2 * pair + i) % PACK * P
                    matmul(acc, q["aff", b, pair // 2], slice(c0, c0 + P), E4M3, q["dyn", b, g], slice(0, W), E5M2, g == 0, g == 1)
                banks.append(acc)
            open_banks["sources", b, pair] = banks

        def store_sources(b, pair, engine):
            result_1 = outs.tile([P, 2, CI], F32, bufs=3)
            dst = out_1[b, block(pair, 2 * P), :].rearrange("(i p) c -> p i c", i=2)
            for i in (1, 0):
                copy(
                    engine,
                    result_1[:, i, :].rearrange("p (r t) -> p r t", t=PACK),
                    open_banks["sources", b, pair][i][:].rearrange("p (t r) -> p r t", t=PACK),
                )
                if b == 1:
                    nc.sync.dma_start(out=dst[:, i, :], in_=result_1[:, i, :])
            if b == 0:
                nc.sync.dma_start(out=dst, in_=result_1[:])

        steps = dict(
            Pf=make_factor, Lg=load_grad, Lw=load_w, Lx=load_gx, La=load_aff, Gs=scale_grad, Gi=group_grad, Gq=quantise_grad, Wi=group_w, Wq=quantise_w, Xt=turn_gx, Xu=untangle_gx,
            Xq=quantise_gx, F=first, D=second, Ri=group_dy, Rq=quantise_dy, Ct=turn_dy, Cu=untangle_dy, Cq=quantise_dyn,
            Ai=group_aff, Aq=quantise_aff, O=rows, Oe=store_rows, S=sources, Se=store_sources,
        )
        for step in PLAN:
            steps[step[0]](*step[1:])
